import numpy as np
import ml_dtypes


def mxq(x, axis, fmt="e4m3"):
    dtype, down = {"e4m3": (ml_dtypes.float8_e4m3fn, 7), "e5m2": (ml_dtypes.float8_e5m2, 14)}[fmt]
    v = np.moveaxis(np.asarray(x, np.float32).astype(ml_dtypes.bfloat16).astype(np.float64), axis, -1)
    blocks = v.reshape(v.shape[:-1] + (-1, 32))
    amax = np.abs(blocks).max(-1, keepdims=True)
    byte = np.maximum(np.where(amax > 0, np.frexp(amax)[1] - 1 + 127, 0) - down, 1)
    scale = np.exp2(byte - 127.0)
    codes = (blocks / scale).astype(np.float32).astype(dtype).astype(np.float64)
    return np.moveaxis((codes * scale).reshape(v.shape), -1, axis)


WIDE = False


def mx_kscale(k):
    if not WIDE:
        return np.ones(k)
    levels = np.array([10, -10, 5, -5, 0])
    if k % 512:
        return np.exp2(np.random.permutation(np.resize(levels, k // 32))).repeat(32)
    a = np.empty((k // 512, 16))
    for p in range(k // 512):
        a[p, :8] = np.random.permutation(np.resize(levels, 8))
        for g in range(8):
            far = levels[np.abs(levels - a[p, g]) >= 10]
            a[p, g + 8] = far[np.random.randint(len(far))]
    return np.exp2(a.ravel()).repeat(32)


BF16 = ml_dtypes.bfloat16


def bf(x):
    return np.asarray(x, np.float32).astype(BF16)


def f64(x):
    return np.asarray(x).astype(np.float64)


L, B, E, H, D, C = 1024, 2, 1024, 8, 128, 512
F = H * D


def rope(z):
    theta = 10000.0 ** (-2.0 / D * np.arange(D // 2))
    ang = np.arange(L)[:, None] * theta[None, :]
    cos, sin = np.cos(ang), np.sin(ang)
    z2 = z.reshape(B, H, L, D // 2, 2)
    r0 = z2[..., 0] * cos - z2[..., 1] * sin
    r1 = z2[..., 0] * sin + z2[..., 1] * cos
    return np.stack([r0, r1], axis=-1).reshape(B, H, L, D)


def setup_inputs():
    s = mx_kscale(E)
    return {"x": bf(np.random.standard_normal((L, B, E)) * s),
            "w": bf(np.random.standard_normal((F, E)) / np.sqrt(E) / s[None, :]),
            "bias": bf(np.random.standard_normal(F) * 0.2)}


def core(x, w, bias):
    y = (mxq(f64(x), 2, "e4m3") @ mxq(f64(w), 1, "e4m3").T) + f64(bias)
    z = y.reshape(L, B, H, D).transpose(1, 2, 0, 3)
    return rope(np.maximum(z, 0.0))


def e4m3fn_bytes(y):
    return np.clip(np.asarray(y, np.float64), -448.0, 448.0).astype(np.float32).astype(ml_dtypes.float8_e4m3fn).view(np.uint8)


def reference(x, w, bias):
    out = core(x, w, bias)
    s = np.max(np.abs(out)) / 448.0
    return out, e4m3fn_bytes(out / s)

@@ -1,0 +1,387 @@
+from contextlib import ExitStack
+
+import concourse.mybir as mybir
+from concourse.masks import make_identity
+
+L, B, E, H, D = 1024, 2, 1024, 8, 128
+FLOPS = 2 * L * B * E * H * D
+
+F32 = mybir.dt.float32
+BF16 = mybir.dt.bfloat16
+I32 = mybir.dt.int32
+U32 = mybir.dt.uint32
+U8 = mybir.dt.uint8
+FP8X4 = mybir.dt.float8_e4m3fn_x4
+FP8 = mybir.dt.float8_e4m3fn
+ALU = mybir.AluOpType
+ACT = mybir.ActivationFunctionType
+AX = mybir.AxisListType
+
+P = 128
+NT = L // P
+PASSES = E // 512
+JT = 4
+HALF = D // 2
+GROUPS = [(0, 0), (1, 0), (0, JT), (1, JT)]
+UNITS = [(g, h) for g in range(len(GROUPS)) for h in range(H)]
+NU = len(UNITS)
+
+TWO_PI = 6.283185307179586
+C1 = 6.28125
+C2 = TWO_PI - C1
+
+MANUAL = True
+VECTOR_SUMS = (NU - 1,)
+ON_SCALAR = (2, 5, 8, 11, 14)
+
+
+def tile_weightlinearattention_pa_kernel(tc, x, w, bias, out_0, out_1):
+    with ExitStack() as top:
+        if MANUAL:
+            top.enter_context(tc.manual_schedule())
+        body(tc, x, w, bias, out_0, out_1)
+
+
+def body(tc, x, w, bias, out_0, out_1):
+    nc = tc.nc
+    x_view = x.rearrange("(p t) c e -> p t c e", t=NT)
+    w_view = w.rearrange("(h d) e -> d h e", d=D)
+
+    with ExitStack() as keep:
+        const = keep.enter_context(tc.tile_pool(name="const", bufs=1))
+        result = keep.enter_context(tc.tile_pool(name="result", bufs=1))
+        psum_misc = keep.enter_context(tc.psum_pool(name="psum_misc", bufs=1))
+
+        slab = {}
+        for c in range(B):
+            for h in range(H):
+                slab[(c, h)] = result.tile([P, NT * D], F32, name="slab_%d_%d" % (c, h))
+        stats = const.tile([P, NU], F32, name="stats")
+
+        with ExitStack() as ph1:
+            xin = ph1.enter_context(tc.tile_pool(name="xin", bufs=1))
+            win = ph1.enter_context(tc.tile_pool(name="win", bufs=1))
+            codes = ph1.enter_context(tc.tile_pool(name="codes", bufs=1))
+            tab = ph1.enter_context(tc.tile_pool(name="tab", bufs=1))
+            stage = ph1.enter_context(tc.tile_pool(name="stage", bufs=4))
+            rpool = ph1.enter_context(tc.tile_pool(name="rpool", bufs=3))
+            prod = ph1.enter_context(tc.tile_pool(name="prod", bufs=3))
+            psum_tp = ph1.enter_context(tc.psum_pool(name="psum_tp", bufs=2))
+            psum_acc = ph1.enter_context(tc.psum_pool(name="psum_acc", bufs=2))
+            psum_bt = ph1.enter_context(tc.psum_pool(name="psum_bt", bufs=3))
+
+            rows_sb = {}
+
+            def load(key):
+                rows_sb[key] = (win if key[0] == "w" else xin).tile([P, E], BF16, name="rows_%s" % "_".join(str(v) for v in key))
+                if key[0] == "w":
+                    nc.sync.dma_start(out=rows_sb[key][:], in_=w_view[:, key[1], :])
+                else:
+                    c, t0 = GROUPS[key[1]]
+                    nc.sync.dma_start(out=rows_sb[key][:], in_=x_view[:, t0 + key[2], c, :])
+
+            load(("w", 0))
+            for j in range(JT):
+                load(("x", 0, j))
+            for h in range(1, H):
+                load(("w", h))
+            for g in range(1, len(GROUPS)):
+                for j in range(JT):
+                    load(("x", g, j))
+
+            bias_rows = const.tile([P, P], BF16, name="bias_rows")
+            nc.vector.memset(bias_rows[:], 0.0)
+            nc.scalar.dma_start(out=bias_rows[0:H, :], in_=bias.rearrange("(h d) -> h d", d=D))
+            warm = const.tile([P, 1], F32, name="warm")
+            nc.vector.memset(warm[:], 0.0)
+            warm_out = const.tile([P, 1], F32, name="warm_out")
+            nc.scalar.activation(out=warm_out[:], in_=warm[:], func=ACT.Sin)
+
+            ident = const.tile([P, P], F32, name="ident")
+            make_identity(nc, ident[:])
+
+            pos = tab.tile([P, NT], F32, name="pos")
+            nc.gpsimd.iota(
+                pos[:], pattern=[[1, NT]], base=0, channel_multiplier=NT, allow_small_or_imprecise_dtypes=True
+            )
+            one = tab.tile([P, 1], F32, name="one")
+            nc.vector.memset(one[:], 1.0)
+            theta = tab.tile([P, HALF], F32, name="theta")
+            for i in range(8):
+                nc.vector.tensor_scalar(
+                    out=theta[:, i : i + 1], in0=one[:], scalar1=10000.0 ** (-2.0 * i / D), scalar2=None, op0=ALU.mult
+                )
+            for n in (8, 16, 32):
+                nc.vector.tensor_scalar(
+                    out=theta[:, n : 2 * n], in0=theta[:, 0:n], scalar1=10000.0 ** (-2.0 * n / D), scalar2=None, op0=ALU.mult
+                )
+
+            halves = (0, 1)
+            shape3 = [P, JT, HALF]
+
+            def tabs(name, dtype=F32):
+                return [tab.tile(shape3, dtype, name="%s_%d" % (name, f)) for f in halves]
+
+            ang = tabs("ang")
+            turns_i = tabs("turns_i", I32)
+            turns = tabs("turns")
+            sin_h = tabs("sin_h")
+            sin_q = tabs("sin_q")
+            sq_h = tabs("sq_h")
+            sq_q = tabs("sq_q")
+            cos_h2 = tabs("cos_h2")
+            cos_t = tabs("cos_t")
+            sin_t = tabs("sin_t")
+            nsin_t = tabs("nsin_t")
+
+            for f in halves:
+                nc.vector.tensor_tensor(
+                    out=ang[f][:],
+                    in0=pos[:, JT * f : JT * (f + 1)].unsqueeze(2).to_broadcast(shape3),
+                    in1=theta[:].unsqueeze(1).to_broadcast(shape3),
+                    op=ALU.mult,
+                )
+            for f in halves:
+                nc.vector.tensor_scalar(
+                    out=turns_i[f][:], in0=ang[f][:], scalar1=1.0 / TWO_PI, scalar2=0.25, op0=ALU.mult, op1=ALU.add
+                )
+            for f in halves:
+                nc.vector.tensor_copy(out=turns[f][:], in_=turns_i[f][:])
+            for part in (C1, C2):
+                for f in halves:
+                    nc.vector.scalar_tensor_tensor(
+                        out=ang[f][:], in0=turns[f][:], scalar=-part, in1=ang[f][:], op0=ALU.mult, op1=ALU.add
+                    )
+            for f in halves:
+                nc.scalar.activation(out=sin_h[f][:], in_=ang[f][:], func=ACT.Sin, scale=0.5)
+                nc.scalar.activation(out=sin_q[f][:], in_=ang[f][:], func=ACT.Sin, scale=0.25)
+
+            def tables(engine, f):
+                engine.tensor_tensor(out=sq_h[f][:], in0=sin_h[f][:], in1=sin_h[f][:], op=ALU.mult)
+                engine.tensor_tensor(out=sq_q[f][:], in0=sin_q[f][:], in1=sin_q[f][:], op=ALU.mult)
+                engine.tensor_scalar(
+                    out=cos_t[f][:], in0=sq_h[f][:], scalar1=-2.0, scalar2=1.0, op0=ALU.mult, op1=ALU.add
+                )
+                engine.tensor_scalar(
+                    out=cos_h2[f][:], in0=sq_q[f][:], scalar1=-4.0, scalar2=2.0, op0=ALU.mult, op1=ALU.add
+                )
+                engine.tensor_tensor(out=sin_t[f][:], in0=sin_h[f][:], in1=cos_h2[f][:], op=ALU.mult)
+                engine.tensor_scalar(
+                    out=nsin_t[f][:], in0=sin_t[f][:], scalar1=-1.0, scalar2=0.0, op0=ALU.mult, op1=ALU.add
+                )
+
+            tables(nc.gpsimd, 1)
+
+            bias_rows_f = const.tile([P, P], F32, name="bias_rows_f")
+            nc.vector.tensor_copy(out=bias_rows_f[:], in_=bias_rows[:])
+            bias_col = const.tile([P, H], F32, name="bias_col")
+
+            x_codes = {}
+            x_scales = {}
+            for g in range(len(GROUPS)):
+                x_codes[g] = codes.tile([P, PASSES, JT * P], U32, name="x_codes_%d" % g, align_bytes=64)
+                x_scales[g] = codes.tile([P, PASSES, JT * P], U8, name="x_scales_%d" % g, align_bytes=64)
+            w_codes = {}
+            w_scales = {}
+            for h in range(H):
+                w_codes[h] = codes.tile([P, PASSES, D], U32, name="w_codes_%d" % h, align_bytes=64)
+                w_scales[h] = codes.tile([P, PASSES, D], U8, name="w_scales_%d" % h, align_bytes=64)
+
+            grouped = {}
+
+            def turn(key):
+                words = rows_sb[key][:].bitcast(F32)
+                bank = psum_tp.tile([P, PASSES, 2, P], F32, name="turn_ps", tag="tp")
+                for s in range(PASSES):
+                    for u in range(2):
+                        nc.tensor.transpose(bank[:, s, u, :], words[:, 256 * s + u : 256 * (s + 1) : 2], ident[:])
+                grouped[key] = stage.tile([P, PASSES, P, 4], BF16, name="grouped", tag="grouped", align_bytes=64)
+                nc.scalar.copy(out=grouped[key][:].bitcast(F32), in_=bank[:].rearrange("p s u r -> p s r u"))
+
+            def quantise(key):
+                if key[0] == "w":
+                    h = key[1]
+                    nc.vector.quantize_mx(
+                        out=w_codes[h][:].rearrange("p s d -> p (s d)").bitcast(FP8X4),
+                        scales=w_scales[h][:].rearrange("p s d -> p (s d)"),
+                        in_=grouped[key][:].rearrange("p s r q -> p (s r q)"),
+                    )
+                else:
+                    g, j = key[1], key[2]
+                    cols = slice(j * P, (j + 1) * P)
+                    for s in range(PASSES):
+                        nc.vector.quantize_mx(
+                            out=x_codes[g][:, s, cols].bitcast(FP8X4),
+                            scales=x_scales[g][:, s, cols],
+                            in_=grouped[key][:, s, :, :].rearrange("p r q -> p (r q)"),
+                        )
+
+            relu = {}
+            back = {}
+            by_cos = {}
+            by_sin = {}
+
+            def multiply(u):
+                g, h = UNITS[u]
+                acc = psum_acc.tile([P, JT * P], F32, name="acc", tag="acc")
+                for s in range(PASSES):
+                    nc.tensor.matmul_mx(
+                        out=acc[:],
+                        lhsT=w_codes[h][:, s, :].bitcast(FP8X4),
+                        lhsT_scale=w_scales[h][:, s, :],
+                        rhs=x_codes[g][:, s, :].bitcast(FP8X4),
+                        rhs_scale=x_scales[g][:, s, :],
+                        start=(s == 0),
+                        stop=(s == PASSES - 1),
+                    )
+                relu[u] = rpool.tile([P, JT * P], F32, name="relu", tag="relu")
+                nc.scalar.activation(out=relu[u][:], in_=acc[:], func=ACT.Relu, bias=bias_col[:, h : h + 1], scale=1.0)
+
+            def turn_back(u):
+                back[u] = psum_bt.tile([P, JT, D], F32, name="back", tag="back")
+                for j in range(JT):
+                    nc.tensor.transpose(back[u][:, j, :], relu[u][:, j * P : (j + 1) * P], ident[:])
+
+            def piece_of(u):
+                g, h = UNITS[u]
+                c, t0 = GROUPS[g]
+                return slab[(c, h)][:, t0 * D : (t0 + JT) * D]
+
+            def times_cos(u):
+                f = GROUPS[UNITS[u][0]][1] // JT
+                planes = back[u][:].rearrange("p j (i e) -> p j e i", e=2)
+                by_cos[u] = prod.tile([P, JT, 2, HALF], F32, name="by_cos", tag="by_cos")
+                nc.vector.tensor_tensor(
+                    out=by_cos[u][:], in0=planes, in1=cos_t[f][:].unsqueeze(2).to_broadcast([P, JT, 2, HALF]), op=ALU.mult
+                )
+
+            def times_sin(u, e):
+                f = GROUPS[UNITS[u][0]][1] // JT
+                planes = back[u][:].rearrange("p j (i e) -> p j e i", e=2)
+                if e == 0:
+                    by_sin[u] = prod.tile([P, JT, 2, HALF], F32, name="by_sin", tag="by_sin")
+                table = nsin_t[f] if e == 0 else sin_t[f]
+                nc.vector.tensor_tensor(out=by_sin[u][:, :, e, :], in0=planes[:, :, 1 - e, :], in1=table[:], op=ALU.mult)
+
+            def add_up(u):
+                engine = nc.vector if u in VECTOR_SUMS else nc.gpsimd
+                engine.tensor_tensor(
+                    out=piece_of(u).rearrange("p (j i e) -> p j i e", j=JT, e=2),
+                    in0=by_cos[u][:].rearrange("p j e i -> p j i e"),
+                    in1=by_sin[u][:].rearrange("p j e i -> p j i e"),
+                    op=ALU.add,
+                )
+
+            def largest(u):
+                nc.vector.tensor_reduce(
+                    out=stats[:, u : u + 1], in_=piece_of(u), axis=AX.X, op=ALU.max, apply_absolute_value=True
+                )
+
+            def store(u):
+                g, h = UNITS[u]
+                c, t0 = GROUPS[g]
+                nc.sync.dma_start(
+                    out=out_0[c, h].rearrange("(p t) d -> p t d", t=NT)[:, t0 : t0 + JT, :],
+                    in_=piece_of(u).rearrange("p (j d) -> p j d", j=JT),
+                )
+
+            turn(("w", 0))
+            turn(("x", 0, 0))
+            tables(nc.vector, 0)
+            quantise(("w", 0))
+            turn(("x", 0, 1))
+            bias_ps = psum_misc.tile([P, P], F32, name="bias_ps", tag="misc")
+            nc.tensor.transpose(bias_ps[:], bias_rows_f[:], ident[:])
+            nc.vector.tensor_copy(out=bias_col[:], in_=bias_ps[:, 0:H])
+            quantise(("x", 0, 0))
+            turn(("x", 0, 2))
+            quantise(("x", 0, 1))
+            turn(("x", 0, 3))
+            quantise(("x", 0, 2))
+            turn(("w", 1))
+            quantise(("x", 0, 3))
+            turn(("w", 2))
+            quantise(("w", 1))
+            multiply(0)
+            quantise(("w", 2))
+            turn(("w", 3))
+            turn_back(0)
+            multiply(1)
+
+            items = {}
+            for h in range(4, H):
+                items.setdefault(h - 4, []).append(("w", h))
+            for g in range(1, len(GROUPS)):
+                for j in range(JT):
+                    items.setdefault(8 * (g - 1) + 1 + j, []).append(("x", g, j))
+            items[-1] = [("w", 3)]
+
+            for k in range(NU + 2):
+                if k + 2 < NU:
+                    multiply(k + 2)
+                if k + 1 < NU:
+                    turn_back(k + 1)
+                for key in items.get(k, []):
+                    turn(key)
+                if 0 <= k - 2:
+                    largest(k - 2)
+                    store(k - 2)
+                if k < NU:
+                    times_cos(k)
+                    times_sin(k, 0)
+                for key in items.get(k - 1, []):
+                    quantise(key)
+                if k < NU:
+                    times_sin(k, 1)
+                    add_up(k)
+
+        with ExitStack() as ph2:
+            scaled = ph2.enter_context(tc.tile_pool(name="scaled", bufs=3))
+            bytes_pool = ph2.enter_context(tc.tile_pool(name="bytes_pool", bufs=1))
+
+            part_max = const.tile([P, 1], F32, name="part_max")
+            nc.vector.tensor_reduce(out=part_max[:], in_=stats[:], axis=AX.X, op=ALU.max)
+            spread = psum_misc.tile([P, P], F32, name="spread", tag="misc")
+            nc.tensor.transpose(spread[:], part_max[:, 0:1].to_broadcast([P, P]), ident[:])
+            amax = const.tile([P, 1], F32, name="amax")
+            nc.vector.tensor_reduce(out=amax[:], in_=spread[:], axis=AX.X, op=ALU.max)
+            recip = const.tile([P, 1], F32, name="recip")
+            nc.vector.reciprocal(out=recip[:], in_=amax[:])
+
+            width = NT * D
+            keys = [(c, h) for c in range(B) for h in range(H)]
+            codes8 = {}
+            sc = {}
+            for n in range(len(keys)):
+                codes8[n] = bytes_pool.tile([P, width], FP8, name="codes8_%d" % n)
+
+            def scale_v(n):
+                sc[n] = scaled.tile([P, width], F32, name="sc_v", tag="sc_v")
+                nc.vector.tensor_scalar(
+                    out=sc[n][:], in0=slab[keys[n]][:], scalar1=recip[:, 0:1], scalar2=448.0, op0=ALU.mult, op1=ALU.mult
+                )
+
+            def cast_v(n):
+                nc.vector.tensor_copy(out=codes8[n][:], in_=sc[n][:], saturate=False)
+
+            def scale_s(n):
+                sc[n] = scaled.tile([P, width], F32, name="sc_s", tag="sc_s")
+                nc.scalar.activation(out=sc[n][:], in_=slab[keys[n]][:], func=ACT.Copy, scale=recip[:, 0:1])
+
+            def cast_s(n):
+                nc.scalar.activation(out=codes8[n][:], in_=sc[n][:], func=ACT.Copy, scale=448.0, saturate=False)
+
+            for scale, cast, mine in (
+                (scale_v, cast_v, [n for n in range(len(keys)) if n not in ON_SCALAR]),
+                (scale_s, cast_s, [n for n in range(len(keys)) if n in ON_SCALAR]),
+            ):
+                scale(mine[0])
+                for a, b in zip(mine[0:], mine[1:]):
+                    scale(b)
+                    cast(a)
+                cast(mine[-1])
+            for n, key in enumerate(keys):
+                c, h = key
+                nc.sync.dma_start(
+                    out=out_1[c, h].rearrange("(p t) d -> p (t d)", t=NT), in_=codes8[n][:].bitcast(U8)
+                )

@@ -220,6 +220,7 @@ def body(tc, x, w, bias, out_0, out_1):
             back = {}
             by_cos = {}
             by_sin = {}
+            summed = {}
 
             def multiply(u):
                 g, h = UNITS[u]
@@ -265,21 +266,25 @@ def body(tc, x, w, bias, out_0, out_1):
 
             def add_up(u):
                 engine = nc.vector if u in VECTOR_SUMS else nc.gpsimd
-                engine.tensor_tensor(
-                    out=piece_of(u).rearrange("p (j i e) -> p j i e", j=JT, e=2),
-                    in0=by_cos[u][:].rearrange("p j e i -> p j i e"),
-                    in1=by_sin[u][:].rearrange("p j e i -> p j i e"),
-                    op=ALU.add,
-                )
+                summed[u] = prod.tile([P, JT, 2, HALF], F32, name="summed", tag="summed", bufs=4)
+                engine.tensor_tensor(out=summed[u][:], in0=by_cos[u][:], in1=by_sin[u][:], op=ALU.add)
 
             def largest(u):
                 nc.vector.tensor_reduce(
-                    out=stats[:, u : u + 1], in_=piece_of(u), axis=AX.X, op=ALU.max, apply_absolute_value=True
+                    out=stats[:, u : u + 1],
+                    in_=summed[u][:].rearrange("p j e i -> p (j e i)"),
+                    axis=AX.X,
+                    op=ALU.max,
+                    apply_absolute_value=True,
                 )
 
             def store(u):
                 g, h = UNITS[u]
                 c, t0 = GROUPS[g]
+                nc.scalar.copy(
+                    out=piece_of(u).rearrange("p (j i e) -> p j i e", j=JT, e=2),
+                    in_=summed[u][:].rearrange("p j e i -> p j i e"),
+                )
                 nc.sync.dma_start(
                     out=out_0[c, h].rearrange("(p t) d -> p t d", t=NT)[:, t0 : t0 + JT, :],
                     in_=piece_of(u).rearrange("p (j d) -> p j d", j=JT),

@@ -31,6 +31,8 @@ C1 = 6.28125
 C2 = TWO_PI - C1
 
 MANUAL = True
+WARM_FIRST = 5
+FILL_FROM = 2
 VECTOR_SUMS = (NU - 1,)
 ON_SCALAR = (2, 5, 8, 11, 14)
 
@@ -89,6 +91,8 @@ def body(tc, x, w, bias, out_0, out_1):
                 for j in range(JT):
                     load(("x", g, j))
 
+            zeros = const.tile([P, P + JT * P], BF16, name="zeros")
+            nc.vector.memset(zeros[:], 0.0)
             bias_rows = const.tile([P, P], BF16, name="bias_rows")
             nc.vector.memset(bias_rows[:], 0.0)
             nc.scalar.dma_start(out=bias_rows[0:H, :], in_=bias.rearrange("(h d) -> h d", d=D))
@@ -99,6 +103,14 @@ def body(tc, x, w, bias, out_0, out_1):
 
             ident = const.tile([P, P], F32, name="ident")
             make_identity(nc, ident[:])
+
+            idle_ps = psum_bt.tile([P, JT * P], F32, name="idle_ps", tag="back")
+
+            def keep_warm(times):
+                for n in range(times):
+                    nc.tensor.matmul(out=idle_ps[:], lhsT=zeros[:, 0:P], rhs=zeros[:, P:], start=True, stop=True)
+
+            keep_warm(WARM_FIRST)
 
             pos = tab.tile([P, NT], F32, name="pos")
             nc.gpsimd.iota(
@@ -218,12 +230,23 @@ def body(tc, x, w, bias, out_0, out_1):
 
             relu = {}
             back = {}
+            idle_mx = []
             by_cos = {}
             by_sin = {}
             summed = {}
 
             def multiply(u):
                 g, h = UNITS[u]
+                if u >= FILL_FROM:
+                    nc.tensor.matmul_mx(
+                        out=idle_mx[0][:],
+                        lhsT=w_codes[h][:, 0, :].bitcast(FP8X4),
+                        lhsT_scale=w_scales[h][:, 0, :],
+                        rhs=x_codes[g][:, 0, :].bitcast(FP8X4),
+                        rhs_scale=x_scales[g][:, 0, :],
+                        start=True,
+                        stop=True,
+                    )
                 acc = psum_acc.tile([P, JT * P], F32, name="acc", tag="acc")
                 for s in range(PASSES):
                     nc.tensor.matmul_mx(
@@ -291,17 +314,23 @@ def body(tc, x, w, bias, out_0, out_1):
                 )
 
             turn(("w", 0))
+            keep_warm(1)
             turn(("x", 0, 0))
+            keep_warm(1)
             tables(nc.vector, 0)
             quantise(("w", 0))
             turn(("x", 0, 1))
+            keep_warm(1)
             bias_ps = psum_misc.tile([P, P], F32, name="bias_ps", tag="misc")
             nc.tensor.transpose(bias_ps[:], bias_rows_f[:], ident[:])
             nc.vector.tensor_copy(out=bias_col[:], in_=bias_ps[:, 0:H])
+            idle_mx.append(psum_misc.tile([P, JT * P], F32, name="idle_mx", tag="misc"))
             quantise(("x", 0, 0))
             turn(("x", 0, 2))
+            keep_warm(1)
             quantise(("x", 0, 1))
             turn(("x", 0, 3))
+            keep_warm(1)
             quantise(("x", 0, 2))
             turn(("w", 1))
             quantise(("x", 0, 3))
@@ -360,31 +389,51 @@ def body(tc, x, w, bias, out_0, out_1):
             for n in range(len(keys)):
                 codes8[n] = bytes_pool.tile([P, width], FP8, name="codes8_%d" % n)
 
-            def scale_v(n):
-                sc[n] = scaled.tile([P, width], F32, name="sc_v", tag="sc_v")
+            def scale_v(n, cols):
+                sc[(n, cols)] = scaled.tile([P, width], F32, name="sc_v", tag="sc_v")
                 nc.vector.tensor_scalar(
-                    out=sc[n][:], in0=slab[keys[n]][:], scalar1=recip[:, 0:1], scalar2=448.0, op0=ALU.mult, op1=ALU.mult
+                    out=sc[(n, cols)][:, cols[0] : cols[1]],
+                    in0=slab[keys[n]][:, cols[0] : cols[1]],
+                    scalar1=recip[:, 0:1],
+                    scalar2=448.0,
+                    op0=ALU.mult,
+                    op1=ALU.mult,
                 )
 
-            def cast_v(n):
-                nc.vector.tensor_copy(out=codes8[n][:], in_=sc[n][:], saturate=False)
+            def cast_v(n, cols):
+                nc.vector.tensor_copy(
+                    out=codes8[n][:, cols[0] : cols[1]], in_=sc[(n, cols)][:, cols[0] : cols[1]], saturate=False
+                )
 
-            def scale_s(n):
-                sc[n] = scaled.tile([P, width], F32, name="sc_s", tag="sc_s")
-                nc.scalar.activation(out=sc[n][:], in_=slab[keys[n]][:], func=ACT.Copy, scale=recip[:, 0:1])
+            def scale_s(n, cols):
+                sc[(n, cols)] = scaled.tile([P, width], F32, name="sc_s", tag="sc_s")
+                nc.scalar.activation(
+                    out=sc[(n, cols)][:, cols[0] : cols[1]],
+                    in_=slab[keys[n]][:, cols[0] : cols[1]],
+                    func=ACT.Copy,
+                    scale=recip[:, 0:1],
+                )
 
-            def cast_s(n):
-                nc.scalar.activation(out=codes8[n][:], in_=sc[n][:], func=ACT.Copy, scale=448.0, saturate=False)
+            def cast_s(n, cols):
+                nc.scalar.activation(
+                    out=codes8[n][:, cols[0] : cols[1]],
+                    in_=sc[(n, cols)][:, cols[0] : cols[1]],
+                    func=ACT.Copy,
+                    scale=448.0,
+                    saturate=False,
+                )
 
+            whole = (0, width)
+            last = len(keys) - 1
             for scale, cast, mine in (
-                (scale_v, cast_v, [n for n in range(len(keys)) if n not in ON_SCALAR]),
-                (scale_s, cast_s, [n for n in range(len(keys)) if n in ON_SCALAR]),
+                (scale_v, cast_v, [(n, whole) for n in range(last) if n not in ON_SCALAR] + [(last, (0, width // 2))]),
+                (scale_s, cast_s, [(n, whole) for n in range(last) if n in ON_SCALAR] + [(last, (width // 2, width))]),
             ):
-                scale(mine[0])
+                scale(mine[0][0], mine[0][1])
                 for a, b in zip(mine[0:], mine[1:]):
-                    scale(b)
-                    cast(a)
-                cast(mine[-1])
+                    scale(b[0], b[1])
+                    cast(a[0], a[1])
+                cast(mine[-1][0], mine[-1][1])
             for n, key in enumerate(keys):
                 c, h = key
                 nc.sync.dma_start(

@@ -30,17 +30,14 @@ TWO_PI = 6.283185307179586
 C1 = 6.28125
 C2 = TWO_PI - C1
 
-MANUAL = True
-WARM_FIRST = 5
-FILL_FROM = 2
+LAG = 3
+LATE_TABLE_STEPS = (6, 7, 8, 9, 14, 15)
 VECTOR_SUMS = (NU - 1,)
 ON_SCALAR = (2, 5, 8, 11, 14)
 
 
 def tile_weightlinearattention_pa_kernel(tc, x, w, bias, out_0, out_1):
-    with ExitStack() as top:
-        if MANUAL:
-            top.enter_context(tc.manual_schedule())
+    with tc.manual_schedule():
         body(tc, x, w, bias, out_0, out_1)
 
 
@@ -67,7 +64,7 @@ def body(tc, x, w, bias, out_0, out_1):
             tab = ph1.enter_context(tc.tile_pool(name="tab", bufs=1))
             stage = ph1.enter_context(tc.tile_pool(name="stage", bufs=4))
             rpool = ph1.enter_context(tc.tile_pool(name="rpool", bufs=3))
-            prod = ph1.enter_context(tc.tile_pool(name="prod", bufs=3))
+            prod = ph1.enter_context(tc.tile_pool(name="prod", bufs=4))
             psum_tp = ph1.enter_context(tc.psum_pool(name="psum_tp", bufs=2))
             psum_acc = ph1.enter_context(tc.psum_pool(name="psum_acc", bufs=2))
             psum_bt = ph1.enter_context(tc.psum_pool(name="psum_bt", bufs=3))
@@ -91,26 +88,16 @@ def body(tc, x, w, bias, out_0, out_1):
                 for j in range(JT):
                     load(("x", g, j))
 
-            zeros = const.tile([P, P + JT * P], BF16, name="zeros")
-            nc.vector.memset(zeros[:], 0.0)
             bias_rows = const.tile([P, P], BF16, name="bias_rows")
-            nc.vector.memset(bias_rows[:], 0.0)
+            nc.gpsimd.memset(bias_rows[:], 0.0)
             nc.scalar.dma_start(out=bias_rows[0:H, :], in_=bias.rearrange("(h d) -> h d", d=D))
             warm = const.tile([P, 1], F32, name="warm")
-            nc.vector.memset(warm[:], 0.0)
+            nc.gpsimd.memset(warm[:], 0.0)
             warm_out = const.tile([P, 1], F32, name="warm_out")
             nc.scalar.activation(out=warm_out[:], in_=warm[:], func=ACT.Sin)
 
             ident = const.tile([P, P], F32, name="ident")
             make_identity(nc, ident[:])
-
-            idle_ps = psum_bt.tile([P, JT * P], F32, name="idle_ps", tag="back")
-
-            def keep_warm(times):
-                for n in range(times):
-                    nc.tensor.matmul(out=idle_ps[:], lhsT=zeros[:, 0:P], rhs=zeros[:, P:], start=True, stop=True)
-
-            keep_warm(WARM_FIRST)
 
             pos = tab.tile([P, NT], F32, name="pos")
             nc.gpsimd.iota(
@@ -168,21 +155,25 @@ def body(tc, x, w, bias, out_0, out_1):
                 nc.scalar.activation(out=sin_h[f][:], in_=ang[f][:], func=ACT.Sin, scale=0.5)
                 nc.scalar.activation(out=sin_q[f][:], in_=ang[f][:], func=ACT.Sin, scale=0.25)
 
-            def tables(engine, f):
-                engine.tensor_tensor(out=sq_h[f][:], in0=sin_h[f][:], in1=sin_h[f][:], op=ALU.mult)
-                engine.tensor_tensor(out=sq_q[f][:], in0=sin_q[f][:], in1=sin_q[f][:], op=ALU.mult)
-                engine.tensor_scalar(
-                    out=cos_t[f][:], in0=sq_h[f][:], scalar1=-2.0, scalar2=1.0, op0=ALU.mult, op1=ALU.add
-                )
-                engine.tensor_scalar(
-                    out=cos_h2[f][:], in0=sq_q[f][:], scalar1=-4.0, scalar2=2.0, op0=ALU.mult, op1=ALU.add
-                )
-                engine.tensor_tensor(out=sin_t[f][:], in0=sin_h[f][:], in1=cos_h2[f][:], op=ALU.mult)
-                engine.tensor_scalar(
-                    out=nsin_t[f][:], in0=sin_t[f][:], scalar1=-1.0, scalar2=0.0, op0=ALU.mult, op1=ALU.add
-                )
-
-            tables(nc.gpsimd, 1)
+            def table_step(engine, f, n):
+                if n == 0:
+                    engine.tensor_tensor(out=sq_h[f][:], in0=sin_h[f][:], in1=sin_h[f][:], op=ALU.mult)
+                elif n == 1:
+                    engine.tensor_tensor(out=sq_q[f][:], in0=sin_q[f][:], in1=sin_q[f][:], op=ALU.mult)
+                elif n == 2:
+                    engine.tensor_scalar(
+                        out=cos_t[f][:], in0=sq_h[f][:], scalar1=-2.0, scalar2=1.0, op0=ALU.mult, op1=ALU.add
+                    )
+                elif n == 3:
+                    engine.tensor_scalar(
+                        out=cos_h2[f][:], in0=sq_q[f][:], scalar1=-4.0, scalar2=2.0, op0=ALU.mult, op1=ALU.add
+                    )
+                elif n == 4:
+                    engine.tensor_tensor(out=sin_t[f][:], in0=sin_h[f][:], in1=cos_h2[f][:], op=ALU.mult)
+                else:
+                    engine.tensor_scalar(
+                        out=nsin_t[f][:], in0=sin_t[f][:], scalar1=-1.0, scalar2=0.0, op0=ALU.mult, op1=ALU.add
+                    )
 
             bias_rows_f = const.tile([P, P], F32, name="bias_rows_f")
             nc.vector.tensor_copy(out=bias_rows_f[:], in_=bias_rows[:])
@@ -191,8 +182,8 @@ def body(tc, x, w, bias, out_0, out_1):
             x_codes = {}
             x_scales = {}
             for g in range(len(GROUPS)):
-                x_codes[g] = codes.tile([P, PASSES, JT * P], U32, name="x_codes_%d" % g, align_bytes=64)
-                x_scales[g] = codes.tile([P, PASSES, JT * P], U8, name="x_scales_%d" % g, align_bytes=64)
+                x_codes[g] = codes.tile([P, JT, PASSES, P], U32, name="x_codes_%d" % g, align_bytes=64)
+                x_scales[g] = codes.tile([P, JT, PASSES, P], U8, name="x_scales_%d" % g, align_bytes=64)
             w_codes = {}
             w_scales = {}
             for h in range(H):
@@ -212,52 +203,35 @@ def body(tc, x, w, bias, out_0, out_1):
 
             def quantise(key):
                 if key[0] == "w":
-                    h = key[1]
-                    nc.vector.quantize_mx(
-                        out=w_codes[h][:].rearrange("p s d -> p (s d)").bitcast(FP8X4),
-                        scales=w_scales[h][:].rearrange("p s d -> p (s d)"),
-                        in_=grouped[key][:].rearrange("p s r q -> p (s r q)"),
-                    )
+                    words, planes = w_codes[key[1]][:], w_scales[key[1]][:]
                 else:
-                    g, j = key[1], key[2]
-                    cols = slice(j * P, (j + 1) * P)
-                    for s in range(PASSES):
-                        nc.vector.quantize_mx(
-                            out=x_codes[g][:, s, cols].bitcast(FP8X4),
-                            scales=x_scales[g][:, s, cols],
-                            in_=grouped[key][:, s, :, :].rearrange("p r q -> p (r q)"),
-                        )
+                    words, planes = x_codes[key[1]][:, key[2], :, :], x_scales[key[1]][:, key[2], :, :]
+                nc.vector.quantize_mx(
+                    out=words.rearrange("p s r -> p (s r)").bitcast(FP8X4),
+                    scales=planes.rearrange("p s r -> p (s r)"),
+                    in_=grouped[key][:].rearrange("p s r q -> p (s r q)"),
+                )
 
             relu = {}
             back = {}
-            idle_mx = []
             by_cos = {}
             by_sin = {}
             summed = {}
 
             def multiply(u):
                 g, h = UNITS[u]
-                if u >= FILL_FROM:
-                    nc.tensor.matmul_mx(
-                        out=idle_mx[0][:],
-                        lhsT=w_codes[h][:, 0, :].bitcast(FP8X4),
-                        lhsT_scale=w_scales[h][:, 0, :],
-                        rhs=x_codes[g][:, 0, :].bitcast(FP8X4),
-                        rhs_scale=x_scales[g][:, 0, :],
-                        start=True,
-                        stop=True,
-                    )
                 acc = psum_acc.tile([P, JT * P], F32, name="acc", tag="acc")
-                for s in range(PASSES):
-                    nc.tensor.matmul_mx(
-                        out=acc[:],
-                        lhsT=w_codes[h][:, s, :].bitcast(FP8X4),
-                        lhsT_scale=w_scales[h][:, s, :],
-                        rhs=x_codes[g][:, s, :].bitcast(FP8X4),
-                        rhs_scale=x_scales[g][:, s, :],
-                        start=(s == 0),
-                        stop=(s == PASSES - 1),
-                    )
+                for j in range(JT):
+                    for s in range(PASSES):
+                        nc.tensor.matmul_mx(
+                            out=acc[:, j * P : (j + 1) * P],
+                            lhsT=w_codes[h][:, s, :].bitcast(FP8X4),
+                            lhsT_scale=w_scales[h][:, s, :],
+                            rhs=x_codes[g][:, j, s, :].bitcast(FP8X4),
+                            rhs_scale=x_scales[g][:, j, s, :],
+                            start=(s == 0),
+                            stop=(s == PASSES - 1),
+                        )
                 relu[u] = rpool.tile([P, JT * P], F32, name="relu", tag="relu")
                 nc.scalar.activation(out=relu[u][:], in_=acc[:], func=ACT.Relu, bias=bias_col[:, h : h + 1], scale=1.0)
 
@@ -289,7 +263,7 @@ def body(tc, x, w, bias, out_0, out_1):
 
             def add_up(u):
                 engine = nc.vector if u in VECTOR_SUMS else nc.gpsimd
-                summed[u] = prod.tile([P, JT, 2, HALF], F32, name="summed", tag="summed", bufs=4)
+                summed[u] = prod.tile([P, JT, 2, HALF], F32, name="summed", tag="summed", bufs=LAG + 3)
                 engine.tensor_tensor(out=summed[u][:], in0=by_cos[u][:], in1=by_sin[u][:], op=ALU.add)
 
             def largest(u):
@@ -314,23 +288,18 @@ def body(tc, x, w, bias, out_0, out_1):
                 )
 
             turn(("w", 0))
-            keep_warm(1)
             turn(("x", 0, 0))
-            keep_warm(1)
-            tables(nc.vector, 0)
+            for n in range(6):
+                table_step(nc.vector, 0, n)
             quantise(("w", 0))
             turn(("x", 0, 1))
-            keep_warm(1)
             bias_ps = psum_misc.tile([P, P], F32, name="bias_ps", tag="misc")
             nc.tensor.transpose(bias_ps[:], bias_rows_f[:], ident[:])
             nc.vector.tensor_copy(out=bias_col[:], in_=bias_ps[:, 0:H])
-            idle_mx.append(psum_misc.tile([P, JT * P], F32, name="idle_mx", tag="misc"))
             quantise(("x", 0, 0))
             turn(("x", 0, 2))
-            keep_warm(1)
             quantise(("x", 0, 1))
             turn(("x", 0, 3))
-            keep_warm(1)
             quantise(("x", 0, 2))
             turn(("w", 1))
             quantise(("x", 0, 3))
@@ -350,24 +319,25 @@ def body(tc, x, w, bias, out_0, out_1):
                     items.setdefault(8 * (g - 1) + 1 + j, []).append(("x", g, j))
             items[-1] = [("w", 3)]
 
-            for k in range(NU + 2):
+            for k in range(NU + LAG):
                 if k + 2 < NU:
                     multiply(k + 2)
                 if k + 1 < NU:
                     turn_back(k + 1)
                 for key in items.get(k, []):
                     turn(key)
-                if 0 <= k - 2:
-                    largest(k - 2)
-                    store(k - 2)
                 if k < NU:
                     times_cos(k)
                     times_sin(k, 0)
-                for key in items.get(k - 1, []):
-                    quantise(key)
-                if k < NU:
                     times_sin(k, 1)
                     add_up(k)
+                if k in LATE_TABLE_STEPS:
+                    table_step(nc.gpsimd, 1, LATE_TABLE_STEPS.index(k))
+                for key in items.get(k - 1, []):
+                    quantise(key)
+                if 0 <= k - LAG:
+                    largest(k - LAG)
+                    store(k - LAG)
 
         with ExitStack() as ph2:
             scaled = ph2.enter_context(tc.tile_pool(name="scaled", bufs=3))

@@ -22,62 +22,66 @@ NT = L // P
 PASSES = E // 512
 JT = 4
 HALF = D // 2
+PLANE = JT * HALF
 GROUPS = [(0, 0), (1, 0), (0, JT), (1, JT)]
 UNITS = [(g, h) for g in range(len(GROUPS)) for h in range(H)]
 NU = len(UNITS)
 
 TWO_PI = 6.283185307179586
-C1 = 6.28125
-C2 = TWO_PI - C1
+TWO_PI_HIGH = 6.28125
+TWO_PI_LOW = TWO_PI - TWO_PI_HIGH
 
 LAG = 3
-LATE_TABLE_STEPS = (6, 7, 8, 9, 14, 15)
-VECTOR_SUMS = (NU - 1,)
-ON_SCALAR = (2, 5, 8, 11, 14)
+
+VECTOR_PIECES = [(0, 0, 2048), (1, 0, 2048), (3, 0, 2048), (4, 0, 2048), (6, 0, 2048), (7, 1024, 1792)]
+SCALAR_PIECES = [(2, 0, 2048), (5, 0, 2048), (7, 0, 1024), (7, 1792, 2048)]
+STORE_ORDER = [(m, a) for m in (0, 1, 2, 3, 5, 4) for a in (0, 1)] + [(7, 0), (6, 0), (6, 1), (7, 1)]
 
 
 def tile_weightlinearattention_pa_kernel(tc, x, w, bias, out_0, out_1):
     with tc.manual_schedule():
-        body(tc, x, w, bias, out_0, out_1)
+        pipeline(tc, x, w, bias, out_0, out_1)
 
 
-def body(tc, x, w, bias, out_0, out_1):
+def pipeline(tc, x, w, bias, out_0, out_1):
     nc = tc.nc
     x_view = x.rearrange("(p t) c e -> p t c e", t=NT)
     w_view = w.rearrange("(h d) e -> d h e", d=D)
 
-    with ExitStack() as keep:
-        const = keep.enter_context(tc.tile_pool(name="const", bufs=1))
-        result = keep.enter_context(tc.tile_pool(name="result", bufs=1))
-        psum_misc = keep.enter_context(tc.psum_pool(name="psum_misc", bufs=1))
+    with ExitStack() as whole_kernel:
+        const = whole_kernel.enter_context(tc.tile_pool(name="const", bufs=1))
+        result = whole_kernel.enter_context(tc.tile_pool(name="result", bufs=1))
+        psum_misc = whole_kernel.enter_context(tc.psum_pool(name="psum_misc", bufs=1))
 
-        slab = {}
-        for c in range(B):
-            for h in range(H):
-                slab[(c, h)] = result.tile([P, NT * D], F32, name="slab_%d_%d" % (c, h))
-        stats = const.tile([P, NU], F32, name="stats")
+        results = [result.tile([P, 2, NT * D], F32, name="results_%d" % m) for m in range(B * H // 2)]
+        largest_of = const.tile([P, NU // 2], F32, name="largest_of")
 
-        with ExitStack() as ph1:
-            xin = ph1.enter_context(tc.tile_pool(name="xin", bufs=1))
-            win = ph1.enter_context(tc.tile_pool(name="win", bufs=1))
-            codes = ph1.enter_context(tc.tile_pool(name="codes", bufs=1))
-            tab = ph1.enter_context(tc.tile_pool(name="tab", bufs=1))
-            stage = ph1.enter_context(tc.tile_pool(name="stage", bufs=4))
-            rpool = ph1.enter_context(tc.tile_pool(name="rpool", bufs=3))
-            prod = ph1.enter_context(tc.tile_pool(name="prod", bufs=4))
-            psum_tp = ph1.enter_context(tc.psum_pool(name="psum_tp", bufs=2))
-            psum_acc = ph1.enter_context(tc.psum_pool(name="psum_acc", bufs=2))
-            psum_bt = ph1.enter_context(tc.psum_pool(name="psum_bt", bufs=3))
+        with ExitStack() as first_phase:
+            xin = first_phase.enter_context(tc.tile_pool(name="xin", bufs=1))
+            win = first_phase.enter_context(tc.tile_pool(name="win", bufs=1))
+            codes = first_phase.enter_context(tc.tile_pool(name="codes", bufs=1))
+            tab = first_phase.enter_context(tc.tile_pool(name="tab", bufs=1))
+            stage = first_phase.enter_context(tc.tile_pool(name="stage", bufs=4))
+            rpool = first_phase.enter_context(tc.tile_pool(name="rpool", bufs=3))
+            prod = first_phase.enter_context(tc.tile_pool(name="prod", bufs=4))
+            psum_tp = first_phase.enter_context(tc.psum_pool(name="psum_tp", bufs=2))
+            psum_acc = first_phase.enter_context(tc.psum_pool(name="psum_acc", bufs=2))
+            psum_bt = first_phase.enter_context(tc.psum_pool(name="psum_bt", bufs=3))
 
-            rows_sb = {}
+            bias_rows = const.tile([P, P], BF16, name="bias_rows")
+            nc.vector.memset(bias_rows[:], 0.0)
+            nc.sync.dma_start(out=bias_rows[0:H, :], in_=bias.rearrange("(h d) -> h d", d=D))
+
+            rows_of = {}
 
             def load(key):
-                rows_sb[key] = (win if key[0] == "w" else xin).tile([P, E], BF16, name="rows_%s" % "_".join(str(v) for v in key))
+                pool = win if key[0] == "w" else xin
+                rows_of[key] = pool.tile([P, E], BF16, name="rows_%s" % "_".join(str(v) for v in key))
                 if key[0] == "w":
-                    nc.sync.dma_start(out=rows_sb[key][:], in_=w_view[:, key[1], :])
+                    nc.sync.dma_start(out=rows_of[key][:], in_=w_view[:, key[1], :])
                 else:
                     c, t0 = GROUPS[key[1]]
-                    nc.sync.dma_start(out=rows_sb[key][:], in_=x_view[:, t0 + key[2], c, :])
+                    nc.sync.dma_start(out=rows_of[key][:], in_=x_view[:, t0 + key[2], c, :])
 
             load(("w", 0))
             for j in range(JT):
@@ -88,21 +92,20 @@ def body(tc, x, w, bias, out_0, out_1):
                 for j in range(JT):
                     load(("x", g, j))
 
-            bias_rows = const.tile([P, P], BF16, name="bias_rows")
-            nc.gpsimd.memset(bias_rows[:], 0.0)
-            nc.scalar.dma_start(out=bias_rows[0:H, :], in_=bias.rearrange("(h d) -> h d", d=D))
-            warm = const.tile([P, 1], F32, name="warm")
-            nc.gpsimd.memset(warm[:], 0.0)
-            warm_out = const.tile([P, 1], F32, name="warm_out")
-            nc.scalar.activation(out=warm_out[:], in_=warm[:], func=ACT.Sin)
+            zeros = const.tile([P, JT * P], BF16, name="zeros")
+            nc.vector.memset(zeros[:], 0.0)
+            zero_col = const.tile([P, 1], F32, name="zero_col")
+            nc.vector.memset(zero_col[:], 0.0)
+            sin_of_zero = const.tile([P, 1], F32, name="sin_of_zero")
+            nc.scalar.activation(out=sin_of_zero[:], in_=zero_col[:], func=ACT.Sin)
 
+            position = tab.tile([P, NT], F32, name="position")
+            nc.gpsimd.iota(
+                position[:], pattern=[[1, NT]], base=0, channel_multiplier=NT, allow_small_or_imprecise_dtypes=True
+            )
             ident = const.tile([P, P], F32, name="ident")
             make_identity(nc, ident[:])
 
-            pos = tab.tile([P, NT], F32, name="pos")
-            nc.gpsimd.iota(
-                pos[:], pattern=[[1, NT]], base=0, channel_multiplier=NT, allow_small_or_imprecise_dtypes=True
-            )
             one = tab.tile([P, 1], F32, name="one")
             nc.vector.memset(one[:], 1.0)
             theta = tab.tile([P, HALF], F32, name="theta")
@@ -110,73 +113,90 @@ def body(tc, x, w, bias, out_0, out_1):
                 nc.vector.tensor_scalar(
                     out=theta[:, i : i + 1], in0=one[:], scalar1=10000.0 ** (-2.0 * i / D), scalar2=None, op0=ALU.mult
                 )
-            for n in (8, 16, 32):
+            for have in (8, 16, 32):
                 nc.vector.tensor_scalar(
-                    out=theta[:, n : 2 * n], in0=theta[:, 0:n], scalar1=10000.0 ** (-2.0 * n / D), scalar2=None, op0=ALU.mult
+                    out=theta[:, have : 2 * have],
+                    in0=theta[:, 0:have],
+                    scalar1=10000.0 ** (-2.0 * have / D),
+                    scalar2=None,
+                    op0=ALU.mult,
                 )
 
             halves = (0, 1)
-            shape3 = [P, JT, HALF]
+            per_half = [P, JT, HALF]
 
-            def tabs(name, dtype=F32):
-                return [tab.tile(shape3, dtype, name="%s_%d" % (name, f)) for f in halves]
+            def two_tiles(name, dtype=F32):
+                return [tab.tile(per_half, dtype, name="%s_%d" % (name, f)) for f in halves]
 
-            ang = tabs("ang")
-            turns_i = tabs("turns_i", I32)
-            turns = tabs("turns")
-            sin_h = tabs("sin_h")
-            sin_q = tabs("sin_q")
-            sq_h = tabs("sq_h")
-            sq_q = tabs("sq_q")
-            cos_h2 = tabs("cos_h2")
-            cos_t = tabs("cos_t")
-            sin_t = tabs("sin_t")
-            nsin_t = tabs("nsin_t")
+            angle = two_tiles("angle")
+            turns_int = two_tiles("turns_int", I32)
+            turns = two_tiles("turns")
+            sin_half = two_tiles("sin_half")
+            sin_quarter = two_tiles("sin_quarter")
+            sq_half = two_tiles("sq_half")
+            sq_quarter = two_tiles("sq_quarter")
+            cos_half_x2 = two_tiles("cos_half_x2")
+            factor = [tab.tile([P, 2, 2, PLANE], F32, name="factor_%d" % f) for f in halves]
 
-            for f in halves:
+            def angles(f):
                 nc.vector.tensor_tensor(
-                    out=ang[f][:],
-                    in0=pos[:, JT * f : JT * (f + 1)].unsqueeze(2).to_broadcast(shape3),
-                    in1=theta[:].unsqueeze(1).to_broadcast(shape3),
+                    out=angle[f][:],
+                    in0=position[:, JT * f : JT * (f + 1)].unsqueeze(2).to_broadcast(per_half),
+                    in1=theta[:].unsqueeze(1).to_broadcast(per_half),
                     op=ALU.mult,
                 )
-            for f in halves:
                 nc.vector.tensor_scalar(
-                    out=turns_i[f][:], in0=ang[f][:], scalar1=1.0 / TWO_PI, scalar2=0.25, op0=ALU.mult, op1=ALU.add
+                    out=turns_int[f][:], in0=angle[f][:], scalar1=1.0 / TWO_PI, scalar2=0.25, op0=ALU.mult, op1=ALU.add
                 )
-            for f in halves:
-                nc.vector.tensor_copy(out=turns[f][:], in_=turns_i[f][:])
-            for part in (C1, C2):
-                for f in halves:
+                nc.vector.tensor_copy(out=turns[f][:], in_=turns_int[f][:])
+
+            def take_turns_off(f):
+                for part in (TWO_PI_HIGH, TWO_PI_LOW):
                     nc.vector.scalar_tensor_tensor(
-                        out=ang[f][:], in0=turns[f][:], scalar=-part, in1=ang[f][:], op0=ALU.mult, op1=ALU.add
-                    )
-            for f in halves:
-                nc.scalar.activation(out=sin_h[f][:], in_=ang[f][:], func=ACT.Sin, scale=0.5)
-                nc.scalar.activation(out=sin_q[f][:], in_=ang[f][:], func=ACT.Sin, scale=0.25)
-
-            def table_step(engine, f, n):
-                if n == 0:
-                    engine.tensor_tensor(out=sq_h[f][:], in0=sin_h[f][:], in1=sin_h[f][:], op=ALU.mult)
-                elif n == 1:
-                    engine.tensor_tensor(out=sq_q[f][:], in0=sin_q[f][:], in1=sin_q[f][:], op=ALU.mult)
-                elif n == 2:
-                    engine.tensor_scalar(
-                        out=cos_t[f][:], in0=sq_h[f][:], scalar1=-2.0, scalar2=1.0, op0=ALU.mult, op1=ALU.add
-                    )
-                elif n == 3:
-                    engine.tensor_scalar(
-                        out=cos_h2[f][:], in0=sq_q[f][:], scalar1=-4.0, scalar2=2.0, op0=ALU.mult, op1=ALU.add
-                    )
-                elif n == 4:
-                    engine.tensor_tensor(out=sin_t[f][:], in0=sin_h[f][:], in1=cos_h2[f][:], op=ALU.mult)
-                else:
-                    engine.tensor_scalar(
-                        out=nsin_t[f][:], in0=sin_t[f][:], scalar1=-1.0, scalar2=0.0, op0=ALU.mult, op1=ALU.add
+                        out=angle[f][:], in0=turns[f][:], scalar=-part, in1=angle[f][:], op0=ALU.mult, op1=ALU.add
                     )
 
-            bias_rows_f = const.tile([P, P], F32, name="bias_rows_f")
-            nc.vector.tensor_copy(out=bias_rows_f[:], in_=bias_rows[:])
+            def sines(f):
+                nc.scalar.activation(out=sin_half[f][:], in_=angle[f][:], func=ACT.Sin, scale=0.5)
+                nc.scalar.activation(out=sin_quarter[f][:], in_=angle[f][:], func=ACT.Sin, scale=0.25)
+
+            def fill_factor(f):
+                flat = "p j i -> p (j i)"
+                nc.gpsimd.tensor_tensor(out=sq_half[f][:], in0=sin_half[f][:], in1=sin_half[f][:], op=ALU.mult)
+                nc.gpsimd.tensor_tensor(out=sq_quarter[f][:], in0=sin_quarter[f][:], in1=sin_quarter[f][:], op=ALU.mult)
+                for e in range(2):
+                    nc.gpsimd.tensor_scalar(
+                        out=factor[f][:, 0, e, :],
+                        in0=sq_half[f][:].rearrange(flat),
+                        scalar1=-2.0,
+                        scalar2=1.0,
+                        op0=ALU.mult,
+                        op1=ALU.add,
+                    )
+                nc.gpsimd.tensor_scalar(
+                    out=cos_half_x2[f][:], in0=sq_quarter[f][:], scalar1=-4.0, scalar2=2.0, op0=ALU.mult, op1=ALU.add
+                )
+                nc.gpsimd.tensor_tensor(
+                    out=factor[f][:, 1, 0, :],
+                    in0=sin_half[f][:].rearrange(flat),
+                    in1=cos_half_x2[f][:].rearrange(flat),
+                    op=ALU.mult,
+                )
+                nc.gpsimd.tensor_scalar(
+                    out=factor[f][:, 1, 1, :],
+                    in0=factor[f][:, 1, 0, :],
+                    scalar1=-1.0,
+                    scalar2=0.0,
+                    op0=ALU.mult,
+                    op1=ALU.add,
+                )
+
+            angles(0)
+            take_turns_off(0)
+            angles(1)
+
+            bias_rows_f32 = const.tile([P, P], F32, name="bias_rows_f32")
+            nc.gpsimd.tensor_copy(out=bias_rows_f32[:], in_=bias_rows[:])
             bias_col = const.tile([P, H], F32, name="bias_col")
 
             x_codes = {}
@@ -192,31 +212,30 @@ def body(tc, x, w, bias, out_0, out_1):
 
             grouped = {}
 
-            def turn(key):
-                words = rows_sb[key][:].bitcast(F32)
-                bank = psum_tp.tile([P, PASSES, 2, P], F32, name="turn_ps", tag="tp")
+            def turn(key, copier=nc.scalar.copy, pool=psum_tp, tag="tp"):
+                words = rows_of[key][:].bitcast(F32)
+                bank = pool.tile([P, PASSES, 2, P], F32, name="turned", tag=tag)
                 for s in range(PASSES):
-                    for u in range(2):
-                        nc.tensor.transpose(bank[:, s, u, :], words[:, 256 * s + u : 256 * (s + 1) : 2], ident[:])
+                    for b in range(2):
+                        nc.tensor.transpose(bank[:, s, b, :], words[:, 256 * s + b : 256 * (s + 1) : 2], ident[:])
                 grouped[key] = stage.tile([P, PASSES, P, 4], BF16, name="grouped", tag="grouped", align_bytes=64)
-                nc.scalar.copy(out=grouped[key][:].bitcast(F32), in_=bank[:].rearrange("p s u r -> p s r u"))
+                copier(out=grouped[key][:].bitcast(F32), in_=bank[:].rearrange("p s b r -> p s r b"))
 
             def quantise(key):
                 if key[0] == "w":
-                    words, planes = w_codes[key[1]][:], w_scales[key[1]][:]
+                    words, scale_bytes = w_codes[key[1]][:], w_scales[key[1]][:]
                 else:
-                    words, planes = x_codes[key[1]][:, key[2], :, :], x_scales[key[1]][:, key[2], :, :]
+                    words, scale_bytes = x_codes[key[1]][:, key[2], :, :], x_scales[key[1]][:, key[2], :, :]
                 nc.vector.quantize_mx(
                     out=words.rearrange("p s r -> p (s r)").bitcast(FP8X4),
-                    scales=planes.rearrange("p s r -> p (s r)"),
+                    scales=scale_bytes.rearrange("p s r -> p (s r)"),
                     in_=grouped[key][:].rearrange("p s r q -> p (s r q)"),
                 )
 
             relu = {}
             back = {}
-            by_cos = {}
-            by_sin = {}
-            summed = {}
+            products = {}
+            sums = {}
 
             def multiply(u):
                 g, h = UNITS[u]
@@ -240,111 +259,120 @@ def body(tc, x, w, bias, out_0, out_1):
                 for j in range(JT):
                     nc.tensor.transpose(back[u][:, j, :], relu[u][:, j * P : (j + 1) * P], ident[:])
 
-            def piece_of(u):
-                g, h = UNITS[u]
-                c, t0 = GROUPS[g]
-                return slab[(c, h)][:, t0 * D : (t0 + JT) * D]
-
-            def times_cos(u):
+            def rotate(u):
                 f = GROUPS[UNITS[u][0]][1] // JT
-                planes = back[u][:].rearrange("p j (i e) -> p j e i", e=2)
-                by_cos[u] = prod.tile([P, JT, 2, HALF], F32, name="by_cos", tag="by_cos")
+                shape = [P, 2, 2, PLANE]
+                planes = back[u][:].rearrange("p j (i e) -> p e (j i)", e=2)
+                if u % 2 == 0:
+                    products[u // 2] = prod.tile([P, 2] + shape[1:], F32, name="products", tag="products", bufs=3)
                 nc.vector.tensor_tensor(
-                    out=by_cos[u][:], in0=planes, in1=cos_t[f][:].unsqueeze(2).to_broadcast([P, JT, 2, HALF]), op=ALU.mult
+                    out=products[u // 2][:, u % 2, :, :, :],
+                    in0=planes.unsqueeze(1).to_broadcast(shape),
+                    in1=factor[f][:],
+                    op=ALU.mult,
                 )
 
-            def times_sin(u, e):
-                f = GROUPS[UNITS[u][0]][1] // JT
-                planes = back[u][:].rearrange("p j (i e) -> p j e i", e=2)
-                if e == 0:
-                    by_sin[u] = prod.tile([P, JT, 2, HALF], F32, name="by_sin", tag="by_sin")
-                table = nsin_t[f] if e == 0 else sin_t[f]
-                nc.vector.tensor_tensor(out=by_sin[u][:, :, e, :], in0=planes[:, :, 1 - e, :], in1=table[:], op=ALU.mult)
+            def add_up(engine, m, which):
+                if m not in sums:
+                    sums[m] = prod.tile([P, 2, 2, PLANE], F32, name="sums", tag="sums")
+                engine.tensor_tensor(
+                    out=sums[m][:, which, :, :],
+                    in0=products[m][:, which, 0, :, :],
+                    in1=products[m][:, which, 1, ::-1, :],
+                    op=ALU.add,
+                )
 
-            def add_up(u):
-                engine = nc.vector if u in VECTOR_SUMS else nc.gpsimd
-                summed[u] = prod.tile([P, JT, 2, HALF], F32, name="summed", tag="summed", bufs=LAG + 3)
-                engine.tensor_tensor(out=summed[u][:], in0=by_cos[u][:], in1=by_sin[u][:], op=ALU.add)
-
-            def largest(u):
+            def largest(m):
                 nc.vector.tensor_reduce(
-                    out=stats[:, u : u + 1],
-                    in_=summed[u][:].rearrange("p j e i -> p (j e i)"),
+                    out=largest_of[:, m : m + 1],
+                    in_=sums[m][:].rearrange("p a e l -> p (a e l)"),
                     axis=AX.X,
                     op=ALU.max,
                     apply_absolute_value=True,
                 )
 
-            def store(u):
-                g, h = UNITS[u]
+            def store(m):
+                g, h = UNITS[2 * m]
                 c, t0 = GROUPS[g]
+                piece = results[(c * H + h) // 2][:, :, t0 * D : (t0 + JT) * D]
                 nc.scalar.copy(
-                    out=piece_of(u).rearrange("p (j i e) -> p j i e", j=JT, e=2),
-                    in_=summed[u][:].rearrange("p j e i -> p j i e"),
+                    out=piece.rearrange("p a (l e) -> p a l e", e=2),
+                    in_=sums[m][:].rearrange("p a e l -> p a l e"),
                 )
                 nc.sync.dma_start(
-                    out=out_0[c, h].rearrange("(p t) d -> p t d", t=NT)[:, t0 : t0 + JT, :],
-                    in_=piece_of(u).rearrange("p (j d) -> p j d", j=JT),
+                    out=out_0[c, h : h + 2].rearrange("a (p t) d -> p a (t d)", t=NT)[:, :, t0 * D : (t0 + JT) * D],
+                    in_=piece,
                 )
 
+            idle_bank = psum_acc.tile([P, JT * P], F32, name="idle_bank", tag="acc")
+
+            def keep_clock_up(times):
+                for repeat in range(times):
+                    nc.tensor.matmul(out=idle_bank[:], lhsT=zeros[:, 0:P], rhs=zeros[:], start=True, stop=True)
+
+            keep_clock_up(3)
+            sines(0)
+            fill_factor(0)
             turn(("w", 0))
-            turn(("x", 0, 0))
-            for n in range(6):
-                table_step(nc.vector, 0, n)
+            turn(("x", 0, 0), copier=nc.vector.tensor_copy)
             quantise(("w", 0))
-            turn(("x", 0, 1))
-            bias_ps = psum_misc.tile([P, P], F32, name="bias_ps", tag="misc")
-            nc.tensor.transpose(bias_ps[:], bias_rows_f[:], ident[:])
-            nc.vector.tensor_copy(out=bias_col[:], in_=bias_ps[:, 0:H])
             quantise(("x", 0, 0))
-            turn(("x", 0, 2))
+            turn(("x", 0, 1), pool=psum_bt, tag="back")
+            keep_clock_up(2)
+            turn(("x", 0, 2), copier=nc.vector.tensor_copy, pool=psum_bt, tag="back")
             quantise(("x", 0, 1))
-            turn(("x", 0, 3))
             quantise(("x", 0, 2))
-            turn(("w", 1))
+            turn(("x", 0, 3), pool=psum_bt, tag="back")
             quantise(("x", 0, 3))
-            turn(("w", 2))
+            bias_bank = psum_misc.tile([P, P], F32, name="bias_bank", tag="misc")
+            nc.tensor.transpose(bias_bank[:], bias_rows_f32[:], ident[:])
+            nc.scalar.copy(out=bias_col[:], in_=bias_bank[:, 0:H])
+            turn(("w", 1), copier=nc.vector.tensor_copy)
             quantise(("w", 1))
-            multiply(0)
+            turn(("w", 2), copier=nc.vector.tensor_copy)
             quantise(("w", 2))
+            take_turns_off(1)
+            multiply(0)
             turn(("w", 3))
+            sines(1)
+            fill_factor(1)
             turn_back(0)
             multiply(1)
 
-            items = {}
+            to_turn = {-1: [("w", 3)]}
             for h in range(4, H):
-                items.setdefault(h - 4, []).append(("w", h))
+                to_turn.setdefault(h - 4, []).append(("w", h))
             for g in range(1, len(GROUPS)):
                 for j in range(JT):
-                    items.setdefault(8 * (g - 1) + 1 + j, []).append(("x", g, j))
-            items[-1] = [("w", 3)]
+                    to_turn.setdefault(H * (g - 1) + 1 + j, []).append(("x", g, j))
 
-            for k in range(NU + LAG):
-                if k + 2 < NU:
-                    multiply(k + 2)
-                if k + 1 < NU:
-                    turn_back(k + 1)
-                for key in items.get(k, []):
+            for step in range(NU + LAG):
+                if step + 2 < NU:
+                    multiply(step + 2)
+                if step + 1 < NU:
+                    turn_back(step + 1)
+                for key in to_turn.get(step, []):
                     turn(key)
-                if k < NU:
-                    times_cos(k)
-                    times_sin(k, 0)
-                    times_sin(k, 1)
-                    add_up(k)
-                if k in LATE_TABLE_STEPS:
-                    table_step(nc.gpsimd, 1, LATE_TABLE_STEPS.index(k))
-                for key in items.get(k - 1, []):
+                if step < NU:
+                    rotate(step)
+                    if step == NU - 2:
+                        add_up(nc.gpsimd, step // 2, slice(0, 1))
+                    elif step == NU - 1:
+                        add_up(nc.vector, step // 2, slice(1, 2))
+                    elif step % 2 == 1:
+                        add_up(nc.gpsimd, step // 2, slice(0, 2))
+                for key in to_turn.get(step - 1, []):
                     quantise(key)
-                if 0 <= k - LAG:
-                    largest(k - LAG)
-                    store(k - LAG)
+                if step >= LAG and (step - LAG) % 2 == 1:
+                    largest((step - LAG) // 2)
+                    store((step - LAG) // 2)
 
-        with ExitStack() as ph2:
-            scaled = ph2.enter_context(tc.tile_pool(name="scaled", bufs=3))
-            bytes_pool = ph2.enter_context(tc.tile_pool(name="bytes_pool", bufs=1))
+        with ExitStack() as second_phase:
+            scaled_pool = second_phase.enter_context(tc.tile_pool(name="scaled_pool", bufs=3))
+            bytes_pool = second_phase.enter_context(tc.tile_pool(name="bytes_pool", bufs=1))
 
             part_max = const.tile([P, 1], F32, name="part_max")
-            nc.vector.tensor_reduce(out=part_max[:], in_=stats[:], axis=AX.X, op=ALU.max)
+            nc.vector.tensor_reduce(out=part_max[:], in_=largest_of[:], axis=AX.X, op=ALU.max)
             spread = psum_misc.tile([P, P], F32, name="spread", tag="misc")
             nc.tensor.transpose(spread[:], part_max[:, 0:1].to_broadcast([P, P]), ident[:])
             amax = const.tile([P, 1], F32, name="amax")
@@ -352,60 +380,57 @@ def body(tc, x, w, bias, out_0, out_1):
             recip = const.tile([P, 1], F32, name="recip")
             nc.vector.reciprocal(out=recip[:], in_=amax[:])
 
-            width = NT * D
-            keys = [(c, h) for c in range(B) for h in range(H)]
-            codes8 = {}
-            sc = {}
-            for n in range(len(keys)):
-                codes8[n] = bytes_pool.tile([P, width], FP8, name="codes8_%d" % n)
+            codes8 = [bytes_pool.tile([P, 2, NT * D], FP8, name="codes8_%d" % m) for m in range(len(results))]
+            scaled = {}
 
-            def scale_v(n, cols):
-                sc[(n, cols)] = scaled.tile([P, width], F32, name="sc_v", tag="sc_v")
+            def columns(pair_tile, piece):
+                return pair_tile[:].rearrange("p a l -> p (a l)")[:, piece[1] : piece[2]]
+
+            def scale_on_vector(piece):
+                scaled[piece] = scaled_pool.tile([P, 2, NT * D], F32, name="scaled_v", tag="scaled_v")
                 nc.vector.tensor_scalar(
-                    out=sc[(n, cols)][:, cols[0] : cols[1]],
-                    in0=slab[keys[n]][:, cols[0] : cols[1]],
+                    out=columns(scaled[piece], piece),
+                    in0=columns(results[piece[0]], piece),
                     scalar1=recip[:, 0:1],
                     scalar2=448.0,
                     op0=ALU.mult,
                     op1=ALU.mult,
                 )
 
-            def cast_v(n, cols):
+            def cast_on_vector(piece):
                 nc.vector.tensor_copy(
-                    out=codes8[n][:, cols[0] : cols[1]], in_=sc[(n, cols)][:, cols[0] : cols[1]], saturate=False
+                    out=columns(codes8[piece[0]], piece), in_=columns(scaled[piece], piece), saturate=False
                 )
 
-            def scale_s(n, cols):
-                sc[(n, cols)] = scaled.tile([P, width], F32, name="sc_s", tag="sc_s")
+            def scale_on_scalar(piece):
+                scaled[piece] = scaled_pool.tile([P, 2, NT * D], F32, name="scaled_s", tag="scaled_s")
                 nc.scalar.activation(
-                    out=sc[(n, cols)][:, cols[0] : cols[1]],
-                    in_=slab[keys[n]][:, cols[0] : cols[1]],
+                    out=columns(scaled[piece], piece),
+                    in_=columns(results[piece[0]], piece),
                     func=ACT.Copy,
                     scale=recip[:, 0:1],
                 )
 
-            def cast_s(n, cols):
+            def cast_on_scalar(piece):
                 nc.scalar.activation(
-                    out=codes8[n][:, cols[0] : cols[1]],
-                    in_=sc[(n, cols)][:, cols[0] : cols[1]],
+                    out=columns(codes8[piece[0]], piece),
+                    in_=columns(scaled[piece], piece),
                     func=ACT.Copy,
                     scale=448.0,
                     saturate=False,
                 )
 
-            whole = (0, width)
-            last = len(keys) - 1
-            for scale, cast, mine in (
-                (scale_v, cast_v, [(n, whole) for n in range(last) if n not in ON_SCALAR] + [(last, (0, width // 2))]),
-                (scale_s, cast_s, [(n, whole) for n in range(last) if n in ON_SCALAR] + [(last, (width // 2, width))]),
+            for scale, cast, pieces in (
+                (scale_on_vector, cast_on_vector, VECTOR_PIECES),
+                (scale_on_scalar, cast_on_scalar, SCALAR_PIECES),
             ):
-                scale(mine[0][0], mine[0][1])
-                for a, b in zip(mine[0:], mine[1:]):
-                    scale(b[0], b[1])
-                    cast(a[0], a[1])
-                cast(mine[-1][0], mine[-1][1])
-            for n, key in enumerate(keys):
-                c, h = key
+                scale(pieces[0])
+                for done, following in zip(pieces[0:], pieces[1:]):
+                    scale(following)
+                    cast(done)
+                cast(pieces[-1])
+            for m, a in STORE_ORDER:
                 nc.sync.dma_start(
-                    out=out_1[c, h].rearrange("(p t) d -> p (t d)", t=NT), in_=codes8[n][:].bitcast(U8)
+                    out=out_1[(2 * m + a) // H, (2 * m + a) % H].rearrange("(p t) d -> p (t d)", t=NT),
+                    in_=codes8[m][:, a, :].bitcast(U8),
                 )

from contextlib import ExitStack

import concourse.mybir as mybir
from concourse.masks import make_identity

L, B, E, H, D = 1024, 2, 1024, 8, 128
FLOPS = 2 * L * B * E * H * D

F32 = mybir.dt.float32
BF16 = mybir.dt.bfloat16
I32 = mybir.dt.int32
U32 = mybir.dt.uint32
U8 = mybir.dt.uint8
FP8X4 = mybir.dt.float8_e4m3fn_x4
FP8 = mybir.dt.float8_e4m3fn
ALU = mybir.AluOpType
ACT = mybir.ActivationFunctionType
AX = mybir.AxisListType

P = 128
NT = L // P
PASSES = E // 512
JT = 4
HALF = D // 2
PLANE = JT * HALF
GROUPS = [(0, 0), (1, 0), (0, JT), (1, JT)]
UNITS = [(g, h) for g in range(len(GROUPS)) for h in range(H)]
NU = len(UNITS)

TWO_PI = 6.283185307179586
TWO_PI_HIGH = 6.28125
TWO_PI_LOW = TWO_PI - TWO_PI_HIGH

LAG = 3

VECTOR_PIECES = [(0, 0, 2048), (1, 0, 2048), (3, 0, 2048), (4, 0, 2048), (6, 0, 2048), (7, 1024, 1792)]
SCALAR_PIECES = [(2, 0, 2048), (5, 0, 2048), (7, 0, 1024), (7, 1792, 2048)]
STORE_ORDER = [(m, a) for m in (0, 1, 2, 3, 5, 4) for a in (0, 1)] + [(7, 0), (6, 0), (6, 1), (7, 1)]


def tile_weightlinearattention_pa_kernel(tc, x, w, bias, out_0, out_1):
    with tc.manual_schedule():
        pipeline(tc, x, w, bias, out_0, out_1)


def pipeline(tc, x, w, bias, out_0, out_1):
    nc = tc.nc
    x_view = x.rearrange("(p t) c e -> p t c e", t=NT)
    w_view = w.rearrange("(h d) e -> d h e", d=D)

    with ExitStack() as whole_kernel:
        const = whole_kernel.enter_context(tc.tile_pool(name="const", bufs=1))
        result = whole_kernel.enter_context(tc.tile_pool(name="result", bufs=1))
        psum_misc = whole_kernel.enter_context(tc.psum_pool(name="psum_misc", bufs=1))

        results = [result.tile([P, 2, NT * D], F32, name="results_%d" % m) for m in range(B * H // 2)]
        largest_of = const.tile([P, NU // 2], F32, name="largest_of")

        with ExitStack() as first_phase:
            xin = first_phase.enter_context(tc.tile_pool(name="xin", bufs=1))
            win = first_phase.enter_context(tc.tile_pool(name="win", bufs=1))
            codes = first_phase.enter_context(tc.tile_pool(name="codes", bufs=1))
            tab = first_phase.enter_context(tc.tile_pool(name="tab", bufs=1))
            stage = first_phase.enter_context(tc.tile_pool(name="stage", bufs=4))
            rpool = first_phase.enter_context(tc.tile_pool(name="rpool", bufs=3))
            prod = first_phase.enter_context(tc.tile_pool(name="prod", bufs=4))
            psum_tp = first_phase.enter_context(tc.psum_pool(name="psum_tp", bufs=2))
            psum_acc = first_phase.enter_context(tc.psum_pool(name="psum_acc", bufs=2))
            psum_bt = first_phase.enter_context(tc.psum_pool(name="psum_bt", bufs=3))

            bias_rows = const.tile([P, P], BF16, name="bias_rows")
            nc.vector.memset(bias_rows[:], 0.0)
            nc.sync.dma_start(out=bias_rows[0:H, :], in_=bias.rearrange("(h d) -> h d", d=D))

            rows_of = {}

            def load(key):
                pool = win if key[0] == "w" else xin
                rows_of[key] = pool.tile([P, E], BF16, name="rows_%s" % "_".join(str(v) for v in key))
                if key[0] == "w":
                    nc.sync.dma_start(out=rows_of[key][:], in_=w_view[:, key[1], :])
                else:
                    c, t0 = GROUPS[key[1]]
                    nc.sync.dma_start(out=rows_of[key][:], in_=x_view[:, t0 + key[2], c, :])

            load(("w", 0))
            for j in range(JT):
                load(("x", 0, j))
            for h in range(1, H):
                load(("w", h))
            for g in range(1, len(GROUPS)):
                for j in range(JT):
                    load(("x", g, j))

            zeros = const.tile([P, JT * P], BF16, name="zeros")
            nc.vector.memset(zeros[:], 0.0)
            zero_col = const.tile([P, 1], F32, name="zero_col")
            nc.vector.memset(zero_col[:], 0.0)
            sin_of_zero = const.tile([P, 1], F32, name="sin_of_zero")
            nc.scalar.activation(out=sin_of_zero[:], in_=zero_col[:], func=ACT.Sin)

            position = tab.tile([P, NT], F32, name="position")
            nc.gpsimd.iota(
                position[:], pattern=[[1, NT]], base=0, channel_multiplier=NT, allow_small_or_imprecise_dtypes=True
            )
            ident = const.tile([P, P], F32, name="ident")
            make_identity(nc, ident[:])

            one = tab.tile([P, 1], F32, name="one")
            nc.vector.memset(one[:], 1.0)
            theta = tab.tile([P, HALF], F32, name="theta")
            for i in range(8):
                nc.vector.tensor_scalar(
                    out=theta[:, i : i + 1], in0=one[:], scalar1=10000.0 ** (-2.0 * i / D), scalar2=None, op0=ALU.mult
                )
            for have in (8, 16, 32):
                nc.vector.tensor_scalar(
                    out=theta[:, have : 2 * have],
                    in0=theta[:, 0:have],
                    scalar1=10000.0 ** (-2.0 * have / D),
                    scalar2=None,
                    op0=ALU.mult,
                )

            halves = (0, 1)
            per_half = [P, JT, HALF]

            def two_tiles(name, dtype=F32):
                return [tab.tile(per_half, dtype, name="%s_%d" % (name, f)) for f in halves]

            angle = two_tiles("angle")
            turns_int = two_tiles("turns_int", I32)
            turns = two_tiles("turns")
            sin_half = two_tiles("sin_half")
            sin_quarter = two_tiles("sin_quarter")
            sq_half = two_tiles("sq_half")
            sq_quarter = two_tiles("sq_quarter")
            cos_half_x2 = two_tiles("cos_half_x2")
            factor = [tab.tile([P, 2, 2, PLANE], F32, name="factor_%d" % f) for f in halves]

            def angles(f):
                nc.vector.tensor_tensor(
                    out=angle[f][:],
                    in0=position[:, JT * f : JT * (f + 1)].unsqueeze(2).to_broadcast(per_half),
                    in1=theta[:].unsqueeze(1).to_broadcast(per_half),
                    op=ALU.mult,
                )
                nc.vector.tensor_scalar(
                    out=turns_int[f][:], in0=angle[f][:], scalar1=1.0 / TWO_PI, scalar2=0.25, op0=ALU.mult, op1=ALU.add
                )
                nc.vector.tensor_copy(out=turns[f][:], in_=turns_int[f][:])

            def take_turns_off(f):
                for part in (TWO_PI_HIGH, TWO_PI_LOW):
                    nc.vector.scalar_tensor_tensor(
                        out=angle[f][:], in0=turns[f][:], scalar=-part, in1=angle[f][:], op0=ALU.mult, op1=ALU.add
                    )

            def sines(f):
                nc.scalar.activation(out=sin_half[f][:], in_=angle[f][:], func=ACT.Sin, scale=0.5)
                nc.scalar.activation(out=sin_quarter[f][:], in_=angle[f][:], func=ACT.Sin, scale=0.25)

            def fill_factor(f):
                flat = "p j i -> p (j i)"
                nc.gpsimd.tensor_tensor(out=sq_half[f][:], in0=sin_half[f][:], in1=sin_half[f][:], op=ALU.mult)
                nc.gpsimd.tensor_tensor(out=sq_quarter[f][:], in0=sin_quarter[f][:], in1=sin_quarter[f][:], op=ALU.mult)
                for e in range(2):
                    nc.gpsimd.tensor_scalar(
                        out=factor[f][:, 0, e, :],
                        in0=sq_half[f][:].rearrange(flat),
                        scalar1=-2.0,
                        scalar2=1.0,
                        op0=ALU.mult,
                        op1=ALU.add,
                    )
                nc.gpsimd.tensor_scalar(
                    out=cos_half_x2[f][:], in0=sq_quarter[f][:], scalar1=-4.0, scalar2=2.0, op0=ALU.mult, op1=ALU.add
                )
                nc.gpsimd.tensor_tensor(
                    out=factor[f][:, 1, 0, :],
                    in0=sin_half[f][:].rearrange(flat),
                    in1=cos_half_x2[f][:].rearrange(flat),
                    op=ALU.mult,
                )
                nc.gpsimd.tensor_scalar(
                    out=factor[f][:, 1, 1, :],
                    in0=factor[f][:, 1, 0, :],
                    scalar1=-1.0,
                    scalar2=0.0,
                    op0=ALU.mult,
                    op1=ALU.add,
                )

            angles(0)
            take_turns_off(0)
            angles(1)

            bias_rows_f32 = const.tile([P, P], F32, name="bias_rows_f32")
            nc.gpsimd.tensor_copy(out=bias_rows_f32[:], in_=bias_rows[:])
            bias_col = const.tile([P, H], F32, name="bias_col")

            x_codes = {}
            x_scales = {}
            for g in range(len(GROUPS)):
                x_codes[g] = codes.tile([P, JT, PASSES, P], U32, name="x_codes_%d" % g, align_bytes=64)
                x_scales[g] = codes.tile([P, JT, PASSES, P], U8, name="x_scales_%d" % g, align_bytes=64)
            w_codes = {}
            w_scales = {}
            for h in range(H):
                w_codes[h] = codes.tile([P, PASSES, D], U32, name="w_codes_%d" % h, align_bytes=64)
                w_scales[h] = codes.tile([P, PASSES, D], U8, name="w_scales_%d" % h, align_bytes=64)

            grouped = {}

            def turn(key, copier=nc.scalar.copy, pool=psum_tp, tag="tp"):
                words = rows_of[key][:].bitcast(F32)
                bank = pool.tile([P, PASSES, 2, P], F32, name="turned", tag=tag)
                for s in range(PASSES):
                    for b in range(2):
                        nc.tensor.transpose(bank[:, s, b, :], words[:, 256 * s + b : 256 * (s + 1) : 2], ident[:])
                grouped[key] = stage.tile([P, PASSES, P, 4], BF16, name="grouped", tag="grouped", align_bytes=64)
                copier(out=grouped[key][:].bitcast(F32), in_=bank[:].rearrange("p s b r -> p s r b"))

            def quantise(key):
                if key[0] == "w":
                    words, scale_bytes = w_codes[key[1]][:], w_scales[key[1]][:]
                else:
                    words, scale_bytes = x_codes[key[1]][:, key[2], :, :], x_scales[key[1]][:, key[2], :, :]
                nc.vector.quantize_mx(
                    out=words.rearrange("p s r -> p (s r)").bitcast(FP8X4),
                    scales=scale_bytes.rearrange("p s r -> p (s r)"),
                    in_=grouped[key][:].rearrange("p s r q -> p (s r q)"),
                )

            relu = {}
            back = {}
            products = {}
            sums = {}

            def multiply(u):
                g, h = UNITS[u]
                acc = psum_acc.tile([P, JT * P], F32, name="acc", tag="acc")
                for j in range(JT):
                    for s in range(PASSES):
                        nc.tensor.matmul_mx(
                            out=acc[:, j * P : (j + 1) * P],
                            lhsT=w_codes[h][:, s, :].bitcast(FP8X4),
                            lhsT_scale=w_scales[h][:, s, :],
                            rhs=x_codes[g][:, j, s, :].bitcast(FP8X4),
                            rhs_scale=x_scales[g][:, j, s, :],
                            start=(s == 0),
                            stop=(s == PASSES - 1),
                        )
                relu[u] = rpool.tile([P, JT * P], F32, name="relu", tag="relu")
                nc.scalar.activation(out=relu[u][:], in_=acc[:], func=ACT.Relu, bias=bias_col[:, h : h + 1], scale=1.0)

            def turn_back(u):
                back[u] = psum_bt.tile([P, JT, D], F32, name="back", tag="back")
                for j in range(JT):
                    nc.tensor.transpose(back[u][:, j, :], relu[u][:, j * P : (j + 1) * P], ident[:])

            def rotate(u):
                f = GROUPS[UNITS[u][0]][1] // JT
                shape = [P, 2, 2, PLANE]
                planes = back[u][:].rearrange("p j (i e) -> p e (j i)", e=2)
                if u % 2 == 0:
                    products[u // 2] = prod.tile([P, 2] + shape[1:], F32, name="products", tag="products", bufs=3)
                nc.vector.tensor_tensor(
                    out=products[u // 2][:, u % 2, :, :, :],
                    in0=planes.unsqueeze(1).to_broadcast(shape),
                    in1=factor[f][:],
                    op=ALU.mult,
                )

            def add_up(engine, m, which):
                if m not in sums:
                    sums[m] = prod.tile([P, 2, 2, PLANE], F32, name="sums", tag="sums")
                engine.tensor_tensor(
                    out=sums[m][:, which, :, :],
                    in0=products[m][:, which, 0, :, :],
                    in1=products[m][:, which, 1, ::-1, :],
                    op=ALU.add,
                )

            def largest(m):
                nc.vector.tensor_reduce(
                    out=largest_of[:, m : m + 1],
                    in_=sums[m][:].rearrange("p a e l -> p (a e l)"),
                    axis=AX.X,
                    op=ALU.max,
                    apply_absolute_value=True,
                )

            def store(m):
                g, h = UNITS[2 * m]
                c, t0 = GROUPS[g]
                piece = results[(c * H + h) // 2][:, :, t0 * D : (t0 + JT) * D]
                nc.scalar.copy(
                    out=piece.rearrange("p a (l e) -> p a l e", e=2),
                    in_=sums[m][:].rearrange("p a e l -> p a l e"),
                )
                nc.sync.dma_start(
                    out=out_0[c, h : h + 2].rearrange("a (p t) d -> p a (t d)", t=NT)[:, :, t0 * D : (t0 + JT) * D],
                    in_=piece,
                )

            idle_bank = psum_acc.tile([P, JT * P], F32, name="idle_bank", tag="acc")

            def keep_clock_up(times):
                for repeat in range(times):
                    nc.tensor.matmul(out=idle_bank[:], lhsT=zeros[:, 0:P], rhs=zeros[:], start=True, stop=True)

            keep_clock_up(3)
            sines(0)
            fill_factor(0)
            turn(("w", 0))
            turn(("x", 0, 0), copier=nc.vector.tensor_copy)
            quantise(("w", 0))
            quantise(("x", 0, 0))
            turn(("x", 0, 1), pool=psum_bt, tag="back")
            keep_clock_up(2)
            turn(("x", 0, 2), copier=nc.vector.tensor_copy, pool=psum_bt, tag="back")
            quantise(("x", 0, 1))
            quantise(("x", 0, 2))
            turn(("x", 0, 3), pool=psum_bt, tag="back")
            quantise(("x", 0, 3))
            bias_bank = psum_misc.tile([P, P], F32, name="bias_bank", tag="misc")
            nc.tensor.transpose(bias_bank[:], bias_rows_f32[:], ident[:])
            nc.scalar.copy(out=bias_col[:], in_=bias_bank[:, 0:H])
            turn(("w", 1), copier=nc.vector.tensor_copy)
            quantise(("w", 1))
            turn(("w", 2), copier=nc.vector.tensor_copy)
            quantise(("w", 2))
            take_turns_off(1)
            multiply(0)
            turn(("w", 3))
            sines(1)
            fill_factor(1)
            turn_back(0)
            multiply(1)

            to_turn = {-1: [("w", 3)]}
            for h in range(4, H):
                to_turn.setdefault(h - 4, []).append(("w", h))
            for g in range(1, len(GROUPS)):
                for j in range(JT):
                    to_turn.setdefault(H * (g - 1) + 1 + j, []).append(("x", g, j))

            for step in range(NU + LAG):
                if step + 2 < NU:
                    multiply(step + 2)
                if step + 1 < NU:
                    turn_back(step + 1)
                for key in to_turn.get(step, []):
                    turn(key)
                if step < NU:
                    rotate(step)
                    if step == NU - 2:
                        add_up(nc.gpsimd, step // 2, slice(0, 1))
                    elif step == NU - 1:
                        add_up(nc.vector, step // 2, slice(1, 2))
                    elif step % 2 == 1:
                        add_up(nc.gpsimd, step // 2, slice(0, 2))
                for key in to_turn.get(step - 1, []):
                    quantise(key)
                if step >= LAG and (step - LAG) % 2 == 1:
                    largest((step - LAG) // 2)
                    store((step - LAG) // 2)

        with ExitStack() as second_phase:
            scaled_pool = second_phase.enter_context(tc.tile_pool(name="scaled_pool", bufs=3))
            bytes_pool = second_phase.enter_context(tc.tile_pool(name="bytes_pool", bufs=1))

            part_max = const.tile([P, 1], F32, name="part_max")
            nc.vector.tensor_reduce(out=part_max[:], in_=largest_of[:], axis=AX.X, op=ALU.max)
            spread = psum_misc.tile([P, P], F32, name="spread", tag="misc")
            nc.tensor.transpose(spread[:], part_max[:, 0:1].to_broadcast([P, P]), ident[:])
            amax = const.tile([P, 1], F32, name="amax")
            nc.vector.tensor_reduce(out=amax[:], in_=spread[:], axis=AX.X, op=ALU.max)
            recip = const.tile([P, 1], F32, name="recip")
            nc.vector.reciprocal(out=recip[:], in_=amax[:])

            codes8 = [bytes_pool.tile([P, 2, NT * D], FP8, name="codes8_%d" % m) for m in range(len(results))]
            scaled = {}

            def columns(pair_tile, piece):
                return pair_tile[:].rearrange("p a l -> p (a l)")[:, piece[1] : piece[2]]

            def scale_on_vector(piece):
                scaled[piece] = scaled_pool.tile([P, 2, NT * D], F32, name="scaled_v", tag="scaled_v")
                nc.vector.tensor_scalar(
                    out=columns(scaled[piece], piece),
                    in0=columns(results[piece[0]], piece),
                    scalar1=recip[:, 0:1],
                    scalar2=448.0,
                    op0=ALU.mult,
                    op1=ALU.mult,
                )

            def cast_on_vector(piece):
                nc.vector.tensor_copy(
                    out=columns(codes8[piece[0]], piece), in_=columns(scaled[piece], piece), saturate=False
                )

            def scale_on_scalar(piece):
                scaled[piece] = scaled_pool.tile([P, 2, NT * D], F32, name="scaled_s", tag="scaled_s")
                nc.scalar.activation(
                    out=columns(scaled[piece], piece),
                    in_=columns(results[piece[0]], piece),
                    func=ACT.Copy,
                    scale=recip[:, 0:1],
                )

            def cast_on_scalar(piece):
                nc.scalar.activation(
                    out=columns(codes8[piece[0]], piece),
                    in_=columns(scaled[piece], piece),
                    func=ACT.Copy,
                    scale=448.0,
                    saturate=False,
                )

            for scale, cast, pieces in (
                (scale_on_vector, cast_on_vector, VECTOR_PIECES),
                (scale_on_scalar, cast_on_scalar, SCALAR_PIECES),
            ):
                scale(pieces[0])
                for done, following in zip(pieces[0:], pieces[1:]):
                    scale(following)
                    cast(done)
                cast(pieces[-1])
            for m, a in STORE_ORDER:
                nc.sync.dma_start(
                    out=out_1[(2 * m + a) // H, (2 * m + a) % H].rearrange("(p t) d -> p (t d)", t=NT),
                    in_=codes8[m][:, a, :].bitcast(U8),
                )
